import numpy as np
import ml_dtypes


def mxq(x, axis, fmt="e4m3"):
    dtype, down = {"e4m3": (ml_dtypes.float8_e4m3fn, 7), "e5m2": (ml_dtypes.float8_e5m2, 14)}[fmt]
    v = np.moveaxis(np.asarray(x, np.float32).astype(ml_dtypes.bfloat16).astype(np.float64), axis, -1)
    blocks = v.reshape(v.shape[:-1] + (-1, 32))
    amax = np.abs(blocks).max(-1, keepdims=True)
    byte = np.maximum(np.where(amax > 0, np.frexp(amax)[1] - 1 + 127, 0) - down, 1)
    scale = np.exp2(byte - 127.0)
    codes = (blocks / scale).astype(np.float32).astype(dtype).astype(np.float64)
    return np.moveaxis((codes * scale).reshape(v.shape), -1, axis)


WIDE = False


def mx_kscale(k):
    if not WIDE:
        return np.ones(k)
    levels = np.array([10, -10, 5, -5, 0])
    a = np.random.permutation(np.resize(levels, k // 512 * 4)).reshape(k // 512, 4)
    idx = np.arange(k)
    return np.exp2(a[idx // 512, idx % 128 // 32])


BF16 = ml_dtypes.bfloat16


def bf(x):
    return np.asarray(x, np.float32).astype(BF16)


def f64(x):
    return np.asarray(x).astype(np.float64)


E2M1 = np.array([0.0, 0.5, 1.0, 1.5, 2.0, 3.0, 4.0, 6.0, -0.0, -0.5, -1.0, -1.5, -2.0, -3.0, -4.0, -6.0])


def pack_weight(w, fmt):
    k, n = w.shape
    w = f64(bf(w)).reshape(k // 32, 32, n)
    amax = np.abs(w).max(1)
    if fmt == "e4m3":
        byte = np.frexp(amax)[1] - 1 + 127 - 7
    else:
        mant, ex = np.frexp(amax / 6.0)
        byte = np.where(mant > 0.5, ex, ex - 1) + 127
    byte = np.clip(np.where(amax > 0, byte, 1), 1, 254)
    scaled = (w * np.exp2(127.0 - byte)[:, None, :]).reshape(k, n).astype(np.float32)
    by_word = np.ascontiguousarray(scaled.reshape(k // 512, 128, 4, n).transpose(0, 1, 3, 2))
    if fmt == "e4m3":
        words = by_word.astype(ml_dtypes.float8_e4m3fn).view(np.uint8)
    else:
        c = by_word.astype(ml_dtypes.float4_e2m1fn).view(np.uint8) & 0xF
        words = c[..., 0::2] | (c[..., 1::2] << 4)
    return np.ascontiguousarray(words), np.ascontiguousarray(byte.astype(np.uint8).reshape(k // 512, 16, n))


def unpack_weight(words, scales, fmt):
    g, p, n, _ = words.shape
    if fmt == "e4m3":
        vals = np.ascontiguousarray(words).view(ml_dtypes.float8_e4m3fn).astype(np.float64)
    else:
        nib = np.empty((g, p, n, 4), np.uint8)
        nib[..., 0::2] = words & 0xF
        nib[..., 1::2] = words >> 4
        vals = E2M1[nib]
    vals = vals * np.repeat(np.exp2(scales.astype(np.float64) - 127.0), 8, axis=1)[..., None]
    return vals.transpose(0, 1, 3, 2).reshape(g * 512, n)


def pack4(w):
    words, scales = pack_weight(w, "e2m1")
    return words.reshape(words.shape[0], 128, -1), scales


def unpack4(words, scales):
    return unpack_weight(words.reshape(words.shape[0], 128, -1, 2), scales, "e2m1")


M, D, F = 256, 1024, 4096


def silu(v):
    return v / (1.0 + np.exp(-v))


def setup_inputs():
    s, t = mx_kscale(D), mx_kscale(F)
    x = bf(np.random.standard_normal((M, D)) * s)
    w_gate = np.random.standard_normal((D, F)) * 0.04 / s[:, None]
    w_up = np.random.standard_normal((D, F)) * 0.04 / s[:, None] * t
    w_down = np.random.standard_normal((F, D)) * 0.03 / t[:, None]
    gate_words, gate_scales = pack4(w_gate)
    up_words, up_scales = pack4(w_up)
    down_words, down_scales = pack4(w_down)
    return {"x": x, "gate_words": gate_words, "gate_scales": gate_scales, "up_words": up_words, "up_scales": up_scales,
            "down_words": down_words, "down_scales": down_scales}


def reference(x, gate_words, gate_scales, up_words, up_scales, down_words, down_scales):
    w_gate = unpack4(gate_words, gate_scales)
    w_up = unpack4(up_words, up_scales)
    w_down = unpack4(down_words, down_scales)
    xq = mxq(f64(x), 1, "e4m3")
    g = xq @ w_gate
    u = xq @ w_up
    h = silu(g) * u
    return mxq(h, 1, "e4m3") @ w_down

@@ -1,0 +1,256 @@
+from contextlib import ExitStack
+
+import concourse.mybir as mybir
+from concourse.masks import make_identity
+
+F32 = mybir.dt.float32
+BF16 = mybir.dt.bfloat16
+I32 = mybir.dt.int32
+U32 = mybir.dt.uint32
+U8 = mybir.dt.uint8
+FP8X4 = mybir.dt.float8_e4m3fn_x4
+FP4X4 = mybir.dt.float4_e2m1fn_x4
+SILU = mybir.ActivationFunctionType.Silu
+MULT = mybir.AluOpType.mult
+
+P = 128
+M, D, F = 256, 1024, 4096
+MT = M // P
+GD = D // 512
+NCH = F // 512
+FLOPS = 2 * M * D * F * 2 + 2 * M * F * D
+
+
+def tile_mlp_kernel(tc, x, gate_words, gate_scales, up_words, up_scales, down_words, down_scales, out):
+    nc = tc.nc
+    with ExitStack() as ctx:
+        keep = ctx.enter_context(tc.tile_pool(name="keep", bufs=1))
+        work = ctx.enter_context(tc.tile_pool(name="work", bufs=3))
+        psum = ctx.enter_context(tc.psum_pool(name="psum", bufs=1))
+        ctx.enter_context(tc.manual_schedule())
+
+        x_sb = keep.tile([P, MT, D], BF16, name="x_sb")
+        ident_f = keep.tile([P, P], F32, name="ident_f")
+        ident_b = keep.tile([P, P], BF16, name="ident_b")
+        warm_in = keep.tile([P, 1], F32, name="warm_in")
+        warm_out = keep.tile([P, 1], F32, name="warm_out")
+        xg = keep.tile([P, MT, GD * P * 4], BF16, name="xg", align_bytes=64)
+        xq = keep.tile([P, MT, GD, P], U32, name="xq", align_bytes=64)
+        xs = keep.tile([P, MT, GD, P], U8, name="xs", align_bytes=64)
+
+        groups = [(0, 2), (2, 2), (4, 4)]
+        planes = []
+        for i, (c0, n) in enumerate(groups):
+            planes.append(keep.tile([P, 2, GD, n * 512], U8, name="plane%d" % i, align_bytes=64))
+        plane_d = keep.tile([P, NCH, D], U8, name="plane_d", align_bytes=64)
+
+        words = {}
+        for w in range(2):
+            for cc in range(NCH // 2):
+                words[(w, cc)] = keep.tile([P, GD, 2048], U8, name="words%d_%d" % (w, cc), align_bytes=64)
+        words_d = []
+        for gg in range(NCH // 2):
+            words_d.append(keep.tile([P, 2, 2 * D], U8, name="words_d%d" % gg, align_bytes=64))
+
+        hq = []
+        hs = []
+        for c in range(NCH):
+            hq.append(keep.tile([P, M], U32, name="hq%d" % c, align_bytes=64))
+            hs.append(keep.tile([P, M], U8, name="hs%d" % c, align_bytes=64))
+
+        def zero(plane, pattern):
+            nc.vector.memset(plane[:].rearrange(pattern).bitcast(I32), 0)
+
+        for m in range(MT):
+            nc.scalar.dma_start(out=x_sb[:, m, :], in_=x[m * P : (m + 1) * P, :])
+        nc.gpsimd.memset(warm_in[:], 0.0)
+        make_identity(nc, ident_f[:])
+        make_identity(nc, ident_b[:])
+        nc.scalar.activation(out=warm_out[:], in_=warm_in[:], func=SILU)
+        for i in range(3):
+            zero(planes[i], "p a b c -> p (a b c)")
+
+        w_dram = [gate_words.bitcast(I32), up_words.bitcast(I32)]
+        s_dram = [gate_scales.bitcast(I32), up_scales.bitcast(I32)]
+
+        def load_scales(i, cut):
+            c0, n = groups[i]
+            pl = planes[i][:].bitcast(I32)
+            a, b = c0 * 128, (c0 + n) * 128
+            for w in range(2):
+                if cut == 4:
+                    for r in range(4):
+                        nc.sync.dma_start(
+                            out=pl[r:P:32, w, :, :],
+                            in_=s_dram[w][:, r:16:4, a:b].rearrange("g q n -> q g n"),
+                        )
+                else:
+                    for h in range(2):
+                        for r in range(4):
+                            nc.sync.dma_start(
+                                out=pl[32 * h + r : P : 64, w, :, :],
+                                in_=s_dram[w][:, 4 * h + r : 16 : 8, a:b].rearrange("g q n -> q g n"),
+                            )
+
+        def load_words(cc):
+            for w in range(2):
+                nc.sync.dma_start(
+                    out=words[(w, cc)][:].bitcast(I32),
+                    in_=w_dram[w][:, :, cc * 512 : (cc + 1) * 512].rearrange("g p b -> p g b"),
+                )
+
+        load_scales(0, 4)
+        load_words(0)
+        load_scales(1, 4)
+        load_words(1)
+        load_scales(2, 2)
+        load_words(2)
+        load_words(3)
+
+        for m in range(MT):
+            xw = x_sb[:, m, :].bitcast(F32)
+            xgf = xg[:, m, :].bitcast(F32).rearrange("p (g w u) -> p g w u", g=GD, u=2)
+            for g in range(GD):
+                xt = psum.tile([P, 2, P], F32, name="xt", tag="b%d" % (4 + 2 * m + g))
+                for u in range(2):
+                    nc.tensor.transpose(xt[:, u, :], xw[:, 256 * g + u : 256 * (g + 1) : 2], ident_f[:])
+                src = xt[:].rearrange("p u w -> p w u")
+                if g == 0:
+                    nc.vector.tensor_copy(out=xgf[:, g, :, :], in_=src)
+                else:
+                    nc.scalar.copy(out=xgf[:, g, :, :], in_=src)
+            nc.vector.quantize_mx(
+                out=xq[:, m, :, :].rearrange("p g w -> p (g w)").bitcast(FP8X4),
+                scales=xs[:, m, :, :].rearrange("p g w -> p (g w)"),
+                in_=xg[:, m, :],
+            )
+
+        zero(plane_d, "p a b -> p (a b)")
+        pd = plane_d[:].bitcast(I32)
+        sd = down_scales.bitcast(I32)
+        for h in range(2):
+            for r in range(4):
+                nc.sync.dma_start(
+                    out=pd[32 * h + r : P : 64, :, :],
+                    in_=sd[:, 4 * h + r : 16 : 8, :].rearrange("g q n -> q g n"),
+                )
+        wd = down_words.bitcast(I32)
+        for gg in range(NCH // 2):
+            nc.sync.dma_start(
+                out=words_d[gg][:].bitcast(I32),
+                in_=wd[2 * gg : 2 * gg + 2, :, :].rearrange("g p b -> p g b"),
+            )
+
+        def plane_of(c):
+            for i, (c0, n) in enumerate(groups):
+                if c0 <= c < c0 + n:
+                    return planes[i], (c - c0) * 512
+            raise ValueError("no group")
+
+        h_tiles = {}
+        grp_tiles = {}
+
+        def passes(c, w, bank0):
+            pl, n0 = plane_of(c)
+            wt = words[(w, c // 2)]
+            b0 = (c % 2) * 1024
+            accs = []
+            for m in range(MT):
+                acc = psum.tile([P, 512], F32, name="acc", tag="b%d" % (bank0 + m))
+                for g in range(GD):
+                    nc.tensor.matmul_mx(
+                        out=acc[:],
+                        lhsT=xq[:, m, g, :].bitcast(FP8X4),
+                        lhsT_scale=xs[:, m, g, :],
+                        rhs=wt[:, g, b0 : b0 + 1024].bitcast(FP4X4),
+                        rhs_scale=pl[:, w, g, n0 : n0 + 512],
+                        start=(g == 0),
+                        stop=(g == GD - 1),
+                    )
+                accs.append(acc)
+            return accs
+
+        def quant(c):
+            nc.vector.quantize_mx(
+                out=hq[c][:].bitcast(FP8X4),
+                scales=hs[c][:],
+                in_=grp_tiles[c][:].rearrange("p m w t -> p (m w t)"),
+            )
+
+        def stage1(c, quant_c):
+            pg = passes(c, 0, 0)
+            sil = []
+            for m in range(MT):
+                s = work.tile([P, 4, P], F32, name="sil", tag="sil", bufs=4)
+                nc.scalar.activation(out=s[:], in_=pg[m][:].rearrange("p (q t) -> p t q", t=4), func=SILU)
+                sil.append(s)
+            pu = passes(c, 1, 2)
+            for m in range(MT):
+                h = work.tile([P, 4, P], BF16, name="h", tag="h", bufs=8)
+                nc.vector.tensor_tensor(
+                    out=h[:], in0=pu[m][:].rearrange("p (q t) -> p t q", t=4), in1=sil[m][:], op=MULT
+                )
+                h_tiles[(c, m)] = h
+                if m == 0 and quant_c is not None:
+                    quant(quant_c)
+
+        def transposes(c):
+            pts = []
+            for m in range(MT):
+                pt = psum.tile([P, 4, P], BF16, name="pt", tag="b%d" % (4 + 2 * (c % 2) + m))
+                for t in range(4):
+                    nc.tensor.transpose(pt[:, t, :], h_tiles[(c, m)][:, t, :], ident_b[:])
+                pts.append(pt)
+            return pts
+
+        def regroup(c, pts):
+            grp = work.tile([P, MT, P, 4], BF16, name="grp", tag="grp", bufs=3, align_bytes=64)
+            grp_tiles[c] = grp
+            nc.scalar.copy(out=grp[:, 0, :, :], in_=pts[0][:].rearrange("p t w -> p w t"))
+            nc.vector.tensor_copy(out=grp[:, 1, :, :], in_=pts[1][:].rearrange("p t w -> p w t"))
+
+        for c in range(NCH):
+            stage1(c, c - 2 if c >= 2 else None)
+            if 1 <= c <= NCH - 2:
+                regroup(c - 1, transposes(c - 1))
+
+        outs = {}
+
+        def stage2(m, gs):
+            for n in range(2):
+                if (m, n) not in outs:
+                    outs[(m, n)] = psum.tile([P, 512], F32, name="po", tag="b%d" % (2 * m + n))
+                for g in gs:
+                    nc.tensor.matmul_mx(
+                        out=outs[(m, n)][:],
+                        lhsT=hq[g][:, m * P : (m + 1) * P].bitcast(FP8X4),
+                        lhsT_scale=hs[g][:, m * P : (m + 1) * P],
+                        rhs=words_d[g // 2][:, g % 2, n * 1024 : (n + 1) * 1024].bitcast(FP4X4),
+                        rhs_scale=plane_d[:, g, n * 512 : (n + 1) * 512],
+                        start=(g == 0),
+                        stop=(g == NCH - 1),
+                    )
+
+        def store(m):
+            for n in range(2):
+                o = work.tile([P, 512], F32, name="o", tag="o", bufs=4)
+                if n == 0:
+                    nc.vector.tensor_copy(out=o[:], in_=outs[(m, n)][:])
+                else:
+                    nc.scalar.copy(out=o[:], in_=outs[(m, n)][:])
+                nc.sync.dma_start(out=out[m * P : (m + 1) * P, n * 512 : (n + 1) * 512], in_=o[:])
+
+        early = list(range(NCH - 2))
+        late = [NCH - 2, NCH - 1]
+        stage2(0, early)
+        pts6 = transposes(NCH - 2)
+        pts7 = transposes(NCH - 1)
+        regroup(NCH - 2, pts6)
+        regroup(NCH - 1, pts7)
+        quant(NCH - 2)
+        quant(NCH - 1)
+        stage2(1, early)
+        stage2(0, late)
+        store(0)
+        stage2(1, late)
+        store(1)

@@ -63,6 +63,15 @@ def tile_mlp_kernel(tc, x, gate_words, gate_scales, up_words, up_scales, down_wo
 
         for m in range(MT):
             nc.scalar.dma_start(out=x_sb[:, m, :], in_=x[m * P : (m + 1) * P, :])
+        wz = keep.tile([P, 512], BF16, name="wz")
+        nc.vector.memset(wz[:], 0.0)
+        pdum = psum.tile([P, 512], F32, name="pdum", tag="b0")
+
+        def dummies(n):
+            for i in range(n):
+                nc.tensor.matmul(out=pdum[:], lhsT=wz[:, 0:P], rhs=wz[:], start=True, stop=True)
+
+        dummies(10)
         nc.gpsimd.memset(warm_in[:], 0.0)
         make_identity(nc, ident_f[:])
         make_identity(nc, ident_b[:])
@@ -124,6 +133,8 @@ def tile_mlp_kernel(tc, x, gate_words, gate_scales, up_words, up_scales, down_wo
                 scales=xs[:, m, :, :].rearrange("p g w -> p (g w)"),
                 in_=xg[:, m, :],
             )
+
+        dummies(2)
 
         zero(plane_d, "p a b -> p (a b)")
         pd = plane_d[:].bitcast(I32)

@@ -20,6 +20,9 @@ GD = D // 512
 NCH = F // 512
 FLOPS = 2 * M * D * F * 2 + 2 * M * F * D
 
+DUMMIES_BEFORE = 5
+DUMMIES_AFTER = 1
+
 
 def tile_mlp_kernel(tc, x, gate_words, gate_scales, up_words, up_scales, down_words, down_scales, out):
     nc = tc.nc
@@ -29,25 +32,34 @@ def tile_mlp_kernel(tc, x, gate_words, gate_scales, up_words, up_scales, down_wo
         psum = ctx.enter_context(tc.psum_pool(name="psum", bufs=1))
         ctx.enter_context(tc.manual_schedule())
 
+        taken = []
+
+        def bank(shape, dtype, name):
+            tag = "b%d" % (len(taken) % 8)
+            taken.append(name)
+            return psum.tile(shape, dtype, name=name, tag=tag)
+
         x_sb = keep.tile([P, MT, D], BF16, name="x_sb")
         ident_f = keep.tile([P, P], F32, name="ident_f")
         ident_b = keep.tile([P, P], BF16, name="ident_b")
-        warm_in = keep.tile([P, 1], F32, name="warm_in")
+        wz = keep.tile([P, 512], BF16, name="wz")
         warm_out = keep.tile([P, 1], F32, name="warm_out")
-        xg = keep.tile([P, MT, GD * P * 4], BF16, name="xg", align_bytes=64)
+        xg = keep.tile([P, MT, GD, P * 4], BF16, name="xg", align_bytes=64)
         xq = keep.tile([P, MT, GD, P], U32, name="xq", align_bytes=64)
         xs = keep.tile([P, MT, GD, P], U8, name="xs", align_bytes=64)
 
         groups = [(0, 2), (2, 2), (4, 4)]
-        planes = []
+        planes = {}
         for i, (c0, n) in enumerate(groups):
-            planes.append(keep.tile([P, 2, GD, n * 512], U8, name="plane%d" % i, align_bytes=64))
+            for w in range(2):
+                planes[(i, w)] = keep.tile([P, GD, n * 512], U8, name="plane%d_%d" % (i, w), align_bytes=64)
         plane_d = keep.tile([P, NCH, D], U8, name="plane_d", align_bytes=64)
 
+        pieces = [(0, 1), (1, 1), (2, 2), (4, 2), (6, 2)]
         words = {}
-        for w in range(2):
-            for cc in range(NCH // 2):
-                words[(w, cc)] = keep.tile([P, GD, 2048], U8, name="words%d_%d" % (w, cc), align_bytes=64)
+        for j, (c0, n) in enumerate(pieces):
+            for w in range(2):
+                words[(j, w)] = keep.tile([P, GD, n * 1024], U8, name="words%d_%d" % (j, w), align_bytes=64)
         words_d = []
         for gg in range(NCH // 2):
             words_d.append(keep.tile([P, 2, 2 * D], U8, name="words_d%d" % gg, align_bytes=64))
@@ -58,92 +70,100 @@ def tile_mlp_kernel(tc, x, gate_words, gate_scales, up_words, up_scales, down_wo
             hq.append(keep.tile([P, M], U32, name="hq%d" % c, align_bytes=64))
             hs.append(keep.tile([P, M], U8, name="hs%d" % c, align_bytes=64))
 
-        def zero(plane, pattern):
-            nc.vector.memset(plane[:].rearrange(pattern).bitcast(I32), 0)
+        def zero(plane):
+            nc.vector.memset(plane[:].rearrange("p a b -> p (a b)").bitcast(I32), 0)
+
+        w_dram = [gate_words.bitcast(I32), up_words.bitcast(I32)]
+        s_dram = [gate_scales.bitcast(I32), up_scales.bitcast(I32)]
+
+        def load_scales(i, w, cut):
+            c0, n = groups[i]
+            pl = planes[(i, w)][:].bitcast(I32)
+            a, b = c0 * 128, (c0 + n) * 128
+            if cut == 4:
+                for r in range(4):
+                    nc.sync.dma_start(
+                        out=pl[r:P:32, :, :],
+                        in_=s_dram[w][:, r:16:4, a:b].rearrange("g q n -> q g n"),
+                    )
+            else:
+                for half in range(2):
+                    for r in range(4):
+                        nc.sync.dma_start(
+                            out=pl[32 * half + r : P : 64, :, :],
+                            in_=s_dram[w][:, 4 * half + r : 16 : 8, a:b].rearrange("g q n -> q g n"),
+                        )
+
+        def load_words(j, w):
+            c0, n = pieces[j]
+            nc.sync.dma_start(
+                out=words[(j, w)][:].bitcast(I32),
+                in_=w_dram[w][:, :, c0 * 256 : (c0 + n) * 256].rearrange("g p b -> p g b"),
+            )
 
         for m in range(MT):
             nc.scalar.dma_start(out=x_sb[:, m, :], in_=x[m * P : (m + 1) * P, :])
-        wz = keep.tile([P, 512], BF16, name="wz")
         nc.vector.memset(wz[:], 0.0)
-        pdum = psum.tile([P, 512], F32, name="pdum", tag="b0")
+        make_identity(nc, ident_f[:])
+        nc.scalar.activation(out=warm_out[:], in_=wz[:, 0:1], func=SILU)
+
+        pdum = bank([P, 512], F32, "pdum")
 
         def dummies(n):
             for i in range(n):
                 nc.tensor.matmul(out=pdum[:], lhsT=wz[:, 0:P], rhs=wz[:], start=True, stop=True)
 
-        dummies(10)
-        nc.gpsimd.memset(warm_in[:], 0.0)
-        make_identity(nc, ident_f[:])
-        make_identity(nc, ident_b[:])
-        nc.scalar.activation(out=warm_out[:], in_=warm_in[:], func=SILU)
-        for i in range(3):
-            zero(planes[i], "p a b c -> p (a b c)")
+        dummies(DUMMIES_BEFORE)
 
-        w_dram = [gate_words.bitcast(I32), up_words.bitcast(I32)]
-        s_dram = [gate_scales.bitcast(I32), up_scales.bitcast(I32)]
+        zero(planes[(0, 0)])
+        zero(planes[(0, 1)])
+        nc.vector.tensor_copy(out=ident_b[:], in_=ident_f[:])
+        zero(planes[(1, 0)])
+        zero(planes[(1, 1)])
 
-        def load_scales(i, cut):
-            c0, n = groups[i]
-            pl = planes[i][:].bitcast(I32)
-            a, b = c0 * 128, (c0 + n) * 128
-            for w in range(2):
-                if cut == 4:
-                    for r in range(4):
-                        nc.sync.dma_start(
-                            out=pl[r:P:32, w, :, :],
-                            in_=s_dram[w][:, r:16:4, a:b].rearrange("g q n -> q g n"),
-                        )
-                else:
-                    for h in range(2):
-                        for r in range(4):
-                            nc.sync.dma_start(
-                                out=pl[32 * h + r : P : 64, w, :, :],
-                                in_=s_dram[w][:, 4 * h + r : 16 : 8, a:b].rearrange("g q n -> q g n"),
-                            )
-
-        def load_words(cc):
-            for w in range(2):
-                nc.sync.dma_start(
-                    out=words[(w, cc)][:].bitcast(I32),
-                    in_=w_dram[w][:, :, cc * 512 : (cc + 1) * 512].rearrange("g p b -> p g b"),
-                )
-
-        load_scales(0, 4)
-        load_words(0)
-        load_scales(1, 4)
-        load_words(1)
-        load_scales(2, 2)
-        load_words(2)
-        load_words(3)
+        for w in range(2):
+            load_scales(0, w, 4)
+            load_words(0, w)
+            load_words(1, w)
+        for w in range(2):
+            load_scales(1, w, 4)
+            load_words(2, w)
 
         for m in range(MT):
             xw = x_sb[:, m, :].bitcast(F32)
-            xgf = xg[:, m, :].bitcast(F32).rearrange("p (g w u) -> p g w u", g=GD, u=2)
             for g in range(GD):
-                xt = psum.tile([P, 2, P], F32, name="xt", tag="b%d" % (4 + 2 * m + g))
+                xt = bank([P, 2, P], F32, "xt")
                 for u in range(2):
                     nc.tensor.transpose(xt[:, u, :], xw[:, 256 * g + u : 256 * (g + 1) : 2], ident_f[:])
+                dst = xg[:, m, g, :].bitcast(F32).rearrange("p (w u) -> p w u", u=2)
                 src = xt[:].rearrange("p u w -> p w u")
                 if g == 0:
-                    nc.vector.tensor_copy(out=xgf[:, g, :, :], in_=src)
+                    nc.vector.tensor_copy(out=dst, in_=src)
                 else:
-                    nc.scalar.copy(out=xgf[:, g, :, :], in_=src)
-            nc.vector.quantize_mx(
-                out=xq[:, m, :, :].rearrange("p g w -> p (g w)").bitcast(FP8X4),
-                scales=xs[:, m, :, :].rearrange("p g w -> p (g w)"),
-                in_=xg[:, m, :],
-            )
+                    nc.scalar.copy(out=dst, in_=src)
+            for g in range(GD):
+                nc.vector.quantize_mx(
+                    out=xq[:, m, g, :].bitcast(FP8X4),
+                    scales=xs[:, m, g, :],
+                    in_=xg[:, m, g, :],
+                )
+        dummies(DUMMIES_AFTER)
 
-        dummies(2)
-
-        zero(plane_d, "p a b -> p (a b)")
+        zero(planes[(2, 0)])
+        zero(planes[(2, 1)])
+        zero(plane_d)
+        for w in range(2):
+            load_scales(2, w, 2)
+            load_words(3, w)
+        for w in range(2):
+            load_words(4, w)
         pd = plane_d[:].bitcast(I32)
         sd = down_scales.bitcast(I32)
-        for h in range(2):
+        for half in range(2):
             for r in range(4):
                 nc.sync.dma_start(
-                    out=pd[32 * h + r : P : 64, :, :],
-                    in_=sd[:, 4 * h + r : 16 : 8, :].rearrange("g q n -> q g n"),
+                    out=pd[32 * half + r : P : 64, :, :],
+                    in_=sd[:, 4 * half + r : 16 : 8, :].rearrange("g q n -> q g n"),
                 )
         wd = down_words.bitcast(I32)
         for gg in range(NCH // 2):
@@ -152,29 +172,29 @@ def tile_mlp_kernel(tc, x, gate_words, gate_scales, up_words, up_scales, down_wo
                 in_=wd[2 * gg : 2 * gg + 2, :, :].rearrange("g p b -> p g b"),
             )
 
-        def plane_of(c):
-            for i, (c0, n) in enumerate(groups):
+        def find(table, c):
+            for i, (c0, n) in enumerate(table):
                 if c0 <= c < c0 + n:
-                    return planes[i], (c - c0) * 512
-            raise ValueError("no group")
+                    return i, c - c0
+            raise ValueError("no entry")
 
         h_tiles = {}
         grp_tiles = {}
+        sil_tiles = {}
 
-        def passes(c, w, bank0):
-            pl, n0 = plane_of(c)
-            wt = words[(w, c // 2)]
-            b0 = (c % 2) * 1024
+        def passes(c, w):
+            i, ci = find(groups, c)
+            j, cj = find(pieces, c)
             accs = []
             for m in range(MT):
-                acc = psum.tile([P, 512], F32, name="acc", tag="b%d" % (bank0 + m))
+                acc = bank([P, 512], F32, "acc")
                 for g in range(GD):
                     nc.tensor.matmul_mx(
                         out=acc[:],
                         lhsT=xq[:, m, g, :].bitcast(FP8X4),
                         lhsT_scale=xs[:, m, g, :],
-                        rhs=wt[:, g, b0 : b0 + 1024].bitcast(FP4X4),
-                        rhs_scale=pl[:, w, g, n0 : n0 + 512],
+                        rhs=words[(j, w)][:, g, cj * 1024 : (cj + 1) * 1024].bitcast(FP4X4),
+                        rhs_scale=planes[(i, w)][:, g, ci * 512 : (ci + 1) * 512],
                         start=(g == 0),
                         stop=(g == GD - 1),
                     )
@@ -188,18 +208,19 @@ def tile_mlp_kernel(tc, x, gate_words, gate_scales, up_words, up_scales, down_wo
                 in_=grp_tiles[c][:].rearrange("p m w t -> p (m w t)"),
             )
 
-        def stage1(c, quant_c):
-            pg = passes(c, 0, 0)
-            sil = []
+        def gate(c):
+            pg = passes(c, 0)
             for m in range(MT):
                 s = work.tile([P, 4, P], F32, name="sil", tag="sil", bufs=4)
                 nc.scalar.activation(out=s[:], in_=pg[m][:].rearrange("p (q t) -> p t q", t=4), func=SILU)
-                sil.append(s)
-            pu = passes(c, 1, 2)
+                sil_tiles[(c, m)] = s
+
+        def up(c, quant_c):
+            pu = passes(c, 1)
             for m in range(MT):
                 h = work.tile([P, 4, P], BF16, name="h", tag="h", bufs=8)
                 nc.vector.tensor_tensor(
-                    out=h[:], in0=pu[m][:].rearrange("p (q t) -> p t q", t=4), in1=sil[m][:], op=MULT
+                    out=h[:], in0=pu[m][:].rearrange("p (q t) -> p t q", t=4), in1=sil_tiles[(c, m)][:], op=MULT
                 )
                 h_tiles[(c, m)] = h
                 if m == 0 and quant_c is not None:
@@ -208,7 +229,7 @@ def tile_mlp_kernel(tc, x, gate_words, gate_scales, up_words, up_scales, down_wo
         def transposes(c):
             pts = []
             for m in range(MT):
-                pt = psum.tile([P, 4, P], BF16, name="pt", tag="b%d" % (4 + 2 * (c % 2) + m))
+                pt = bank([P, 4, P], BF16, "pt")
                 for t in range(4):
                     nc.tensor.transpose(pt[:, t, :], h_tiles[(c, m)][:, t, :], ident_b[:])
                 pts.append(pt)
@@ -220,9 +241,15 @@ def tile_mlp_kernel(tc, x, gate_words, gate_scales, up_words, up_scales, down_wo
             nc.scalar.copy(out=grp[:, 0, :, :], in_=pts[0][:].rearrange("p t w -> p w t"))
             nc.vector.tensor_copy(out=grp[:, 1, :, :], in_=pts[1][:].rearrange("p t w -> p w t"))
 
-        for c in range(NCH):
-            stage1(c, c - 2 if c >= 2 else None)
-            if 1 <= c <= NCH - 2:
+        gate(0)
+        gate(1)
+        up(0, None)
+        up(1, None)
+        regroup(0, transposes(0))
+        for c in range(2, NCH):
+            gate(c)
+            up(c, c - 2)
+            if c <= NCH - 2:
                 regroup(c - 1, transposes(c - 1))
 
         outs = {}
@@ -230,7 +257,8 @@ def tile_mlp_kernel(tc, x, gate_words, gate_scales, up_words, up_scales, down_wo
         def stage2(m, gs):
             for n in range(2):
                 if (m, n) not in outs:
-                    outs[(m, n)] = psum.tile([P, 512], F32, name="po", tag="b%d" % (2 * m + n))
+                    outs[(m, n)] = bank([P, 512], F32, "po")
+            for n in range(2):
                 for g in gs:
                     nc.tensor.matmul_mx(
                         out=outs[(m, n)][:],

@@ -229,9 +229,11 @@ def tile_mlp_kernel(tc, x, gate_words, gate_scales, up_words, up_scales, down_wo
         def transposes(c):
             pts = []
             for m in range(MT):
-                pt = bank([P, 4, P], BF16, "pt")
+                pt = bank([P, 4, P], F32, "pt")
                 for t in range(4):
-                    nc.tensor.transpose(pt[:, t, :], h_tiles[(c, m)][:, t, :], ident_b[:])
+                    nc.tensor.matmul(
+                        out=pt[:, t, :], lhsT=h_tiles[(c, m)][:, t, :], rhs=ident_b[:], start=True, stop=True
+                    )
                 pts.append(pt)
             return pts
 

@@ -48,14 +48,16 @@ def tile_mlp_kernel(tc, x, gate_words, gate_scales, up_words, up_scales, down_wo
         xq = keep.tile([P, MT, GD, P], U32, name="xq", align_bytes=64)
         xs = keep.tile([P, MT, GD, P], U8, name="xs", align_bytes=64)
 
-        groups = [(0, 2), (2, 2), (4, 4)]
+        groups = [(0, 2), (2, 2), (4, 2), (6, 2)]
         planes = {}
         for i, (c0, n) in enumerate(groups):
             for w in range(2):
                 planes[(i, w)] = keep.tile([P, GD, n * 512], U8, name="plane%d_%d" % (i, w), align_bytes=64)
-        plane_d = keep.tile([P, NCH, D], U8, name="plane_d", align_bytes=64)
+        planes_d = []
+        for i in range(2):
+            planes_d.append(keep.tile([P, NCH // 2, D], U8, name="plane_d%d" % i, align_bytes=64))
 
-        pieces = [(0, 1), (1, 1), (2, 2), (4, 2), (6, 2)]
+        pieces = [(0, 1), (1, 1), (2, 1), (3, 1), (4, 1), (5, 1), (6, 2)]
         words = {}
         for j, (c0, n) in enumerate(pieces):
             for w in range(2):
@@ -76,23 +78,15 @@ def tile_mlp_kernel(tc, x, gate_words, gate_scales, up_words, up_scales, down_wo
         w_dram = [gate_words.bitcast(I32), up_words.bitcast(I32)]
         s_dram = [gate_scales.bitcast(I32), up_scales.bitcast(I32)]
 
-        def load_scales(i, w, cut):
+        def load_scales(i, w):
             c0, n = groups[i]
             pl = planes[(i, w)][:].bitcast(I32)
             a, b = c0 * 128, (c0 + n) * 128
-            if cut == 4:
-                for r in range(4):
-                    nc.sync.dma_start(
-                        out=pl[r:P:32, :, :],
-                        in_=s_dram[w][:, r:16:4, a:b].rearrange("g q n -> q g n"),
-                    )
-            else:
-                for half in range(2):
-                    for r in range(4):
-                        nc.sync.dma_start(
-                            out=pl[32 * half + r : P : 64, :, :],
-                            in_=s_dram[w][:, 4 * half + r : 16 : 8, a:b].rearrange("g q n -> q g n"),
-                        )
+            for r in range(4):
+                nc.sync.dma_start(
+                    out=pl[r:P:32, :, :],
+                    in_=s_dram[w][:, r:16:4, a:b].rearrange("g q n -> q g n"),
+                )
 
         def load_words(j, w):
             c0, n = pieces[j]
@@ -122,12 +116,14 @@ def tile_mlp_kernel(tc, x, gate_words, gate_scales, up_words, up_scales, down_wo
         zero(planes[(1, 1)])
 
         for w in range(2):
-            load_scales(0, w, 4)
+            load_scales(0, w)
             load_words(0, w)
             load_words(1, w)
         for w in range(2):
-            load_scales(1, w, 4)
+            load_scales(1, w)
             load_words(2, w)
+        for w in range(2):
+            load_words(3, w)
 
         for m in range(MT):
             xw = x_sb[:, m, :].bitcast(F32)
@@ -149,28 +145,33 @@ def tile_mlp_kernel(tc, x, gate_words, gate_scales, up_words, up_scales, down_wo
                 )
         dummies(DUMMIES_AFTER)
 
-        zero(planes[(2, 0)])
-        zero(planes[(2, 1)])
-        zero(plane_d)
+        for i in (2, 3):
+            for w in range(2):
+                zero(planes[(i, w)])
+        for i in range(2):
+            zero(planes_d[i])
         for w in range(2):
-            load_scales(2, w, 2)
-            load_words(3, w)
-        for w in range(2):
+            load_scales(2, w)
             load_words(4, w)
-        pd = plane_d[:].bitcast(I32)
+        for w in range(2):
+            load_words(5, w)
+        for w in range(2):
+            load_scales(3, w)
+            load_words(6, w)
         sd = down_scales.bitcast(I32)
-        for half in range(2):
+        wd = down_words.bitcast(I32)
+        for i in range(2):
+            pd = planes_d[i][:].bitcast(I32)
             for r in range(4):
                 nc.sync.dma_start(
-                    out=pd[32 * half + r : P : 64, :, :],
-                    in_=sd[:, 4 * half + r : 16 : 8, :].rearrange("g q n -> q g n"),
+                    out=pd[r:P:32, :, :],
+                    in_=sd[4 * i : 4 * i + 4, r:16:4, :].rearrange("g q n -> q g n"),
                 )
-        wd = down_words.bitcast(I32)
-        for gg in range(NCH // 2):
-            nc.sync.dma_start(
-                out=words_d[gg][:].bitcast(I32),
-                in_=wd[2 * gg : 2 * gg + 2, :, :].rearrange("g p b -> p g b"),
-            )
+            for gg in (2 * i, 2 * i + 1):
+                nc.sync.dma_start(
+                    out=words_d[gg][:].bitcast(I32),
+                    in_=wd[2 * gg : 2 * gg + 2, :, :].rearrange("g p b -> p g b"),
+                )
 
         def find(table, c):
             for i, (c0, n) in enumerate(table):
@@ -229,11 +230,9 @@ def tile_mlp_kernel(tc, x, gate_words, gate_scales, up_words, up_scales, down_wo
         def transposes(c):
             pts = []
             for m in range(MT):
-                pt = bank([P, 4, P], F32, "pt")
+                pt = bank([P, 4, P], BF16, "pt")
                 for t in range(4):
-                    nc.tensor.matmul(
-                        out=pt[:, t, :], lhsT=h_tiles[(c, m)][:, t, :], rhs=ident_b[:], start=True, stop=True
-                    )
+                    nc.tensor.transpose(pt[:, t, :], h_tiles[(c, m)][:, t, :], ident_b[:])
                 pts.append(pt)
             return pts
 
@@ -260,14 +259,14 @@ def tile_mlp_kernel(tc, x, gate_words, gate_scales, up_words, up_scales, down_wo
             for n in range(2):
                 if (m, n) not in outs:
                     outs[(m, n)] = bank([P, 512], F32, "po")
-            for n in range(2):
-                for g in gs:
+            for g in gs:
+                for n in range(2):
                     nc.tensor.matmul_mx(
                         out=outs[(m, n)][:],
                         lhsT=hq[g][:, m * P : (m + 1) * P].bitcast(FP8X4),
                         lhsT_scale=hs[g][:, m * P : (m + 1) * P],
                         rhs=words_d[g // 2][:, g % 2, n * 1024 : (n + 1) * 1024].bitcast(FP4X4),
-                        rhs_scale=plane_d[:, g, n * 512 : (n + 1) * 512],
+                        rhs_scale=planes_d[g // 4][:, g % 4, n * 512 : (n + 1) * 512],
                         start=(g == 0),
                         stop=(g == NCH - 1),
                     )
@@ -281,8 +280,8 @@ def tile_mlp_kernel(tc, x, gate_words, gate_scales, up_words, up_scales, down_wo
                     nc.scalar.copy(out=o[:], in_=outs[(m, n)][:])
                 nc.sync.dma_start(out=out[m * P : (m + 1) * P, n * 512 : (n + 1) * 512], in_=o[:])
 
-        early = list(range(NCH - 2))
-        late = [NCH - 2, NCH - 1]
+        early = list(range(NCH // 2))
+        late = list(range(NCH // 2, NCH))
         stage2(0, early)
         pts6 = transposes(NCH - 2)
         pts7 = transposes(NCH - 1)

@@ -216,7 +216,7 @@ def tile_mlp_kernel(tc, x, gate_words, gate_scales, up_words, up_scales, down_wo
                 nc.scalar.activation(out=s[:], in_=pg[m][:].rearrange("p (q t) -> p t q", t=4), func=SILU)
                 sil_tiles[(c, m)] = s
 
-        def up(c, quant_c):
+        def up(c):
             pu = passes(c, 1)
             for m in range(MT):
                 h = work.tile([P, 4, P], BF16, name="h", tag="h", bufs=8)
@@ -224,8 +224,6 @@ def tile_mlp_kernel(tc, x, gate_words, gate_scales, up_words, up_scales, down_wo
                     out=h[:], in0=pu[m][:].rearrange("p (q t) -> p t q", t=4), in1=sil_tiles[(c, m)][:], op=MULT
                 )
                 h_tiles[(c, m)] = h
-                if m == 0 and quant_c is not None:
-                    quant(quant_c)
 
         def transposes(c):
             pts = []
@@ -237,21 +235,28 @@ def tile_mlp_kernel(tc, x, gate_words, gate_scales, up_words, up_scales, down_wo
             return pts
 
         def regroup(c, pts):
-            grp = work.tile([P, MT, P, 4], BF16, name="grp", tag="grp", bufs=3, align_bytes=64)
+            grp = work.tile([P, MT, P, 4], BF16, name="grp", tag="grp", bufs=4, align_bytes=64)
             grp_tiles[c] = grp
             nc.scalar.copy(out=grp[:, 0, :, :], in_=pts[0][:].rearrange("p t w -> p w t"))
             nc.vector.tensor_copy(out=grp[:, 1, :, :], in_=pts[1][:].rearrange("p t w -> p w t"))
 
+        def turn(a, b):
+            pts_a = transposes(a)
+            pts_b = transposes(b)
+            regroup(a, pts_a)
+            regroup(b, pts_b)
+            quant(a)
+            quant(b)
+
         gate(0)
         gate(1)
-        up(0, None)
-        up(1, None)
-        regroup(0, transposes(0))
+        up(0)
+        up(1)
         for c in range(2, NCH):
             gate(c)
-            up(c, c - 2)
-            if c <= NCH - 2:
-                regroup(c - 1, transposes(c - 1))
+            up(c)
+            if c % 2 == 0:
+                turn(c - 2, c - 1)
 
         outs = {}
 
@@ -283,12 +288,7 @@ def tile_mlp_kernel(tc, x, gate_words, gate_scales, up_words, up_scales, down_wo
         early = list(range(NCH // 2))
         late = list(range(NCH // 2, NCH))
         stage2(0, early)
-        pts6 = transposes(NCH - 2)
-        pts7 = transposes(NCH - 1)
-        regroup(NCH - 2, pts6)
-        regroup(NCH - 1, pts7)
-        quant(NCH - 2)
-        quant(NCH - 1)
+        turn(NCH - 2, NCH - 1)
         stage2(1, early)
         stage2(0, late)
         store(0)

@@ -115,10 +115,13 @@ def tile_mlp_kernel(tc, x, gate_words, gate_scales, up_words, up_scales, down_wo
         zero(planes[(1, 0)])
         zero(planes[(1, 1)])
 
-        for w in range(2):
-            load_scales(0, w)
-            load_words(0, w)
-            load_words(1, w)
+        load_scales(0, 0)
+        for g in range(GD):
+            nc.sync.dma_start(out=words[(0, 0)][:, g, :].bitcast(I32), in_=w_dram[0][g, :, 0:256])
+        load_words(1, 0)
+        load_scales(0, 1)
+        load_words(0, 1)
+        load_words(1, 1)
         for w in range(2):
             load_scales(1, w)
             load_words(2, w)
@@ -216,7 +219,7 @@ def tile_mlp_kernel(tc, x, gate_words, gate_scales, up_words, up_scales, down_wo
                 nc.scalar.activation(out=s[:], in_=pg[m][:].rearrange("p (q t) -> p t q", t=4), func=SILU)
                 sil_tiles[(c, m)] = s
 
-        def up(c):
+        def up(c, quant_c):
             pu = passes(c, 1)
             for m in range(MT):
                 h = work.tile([P, 4, P], BF16, name="h", tag="h", bufs=8)
@@ -224,6 +227,8 @@ def tile_mlp_kernel(tc, x, gate_words, gate_scales, up_words, up_scales, down_wo
                     out=h[:], in0=pu[m][:].rearrange("p (q t) -> p t q", t=4), in1=sil_tiles[(c, m)][:], op=MULT
                 )
                 h_tiles[(c, m)] = h
+                if m == 0 and quant_c is not None:
+                    quant(quant_c)
 
         def transposes(c):
             pts = []
@@ -235,37 +240,30 @@ def tile_mlp_kernel(tc, x, gate_words, gate_scales, up_words, up_scales, down_wo
             return pts
 
         def regroup(c, pts):
-            grp = work.tile([P, MT, P, 4], BF16, name="grp", tag="grp", bufs=4, align_bytes=64)
+            grp = work.tile([P, MT, P, 4], BF16, name="grp", tag="grp", bufs=3, align_bytes=64)
             grp_tiles[c] = grp
             nc.scalar.copy(out=grp[:, 0, :, :], in_=pts[0][:].rearrange("p t w -> p w t"))
             nc.vector.tensor_copy(out=grp[:, 1, :, :], in_=pts[1][:].rearrange("p t w -> p w t"))
 
-        def turn(a, b):
-            pts_a = transposes(a)
-            pts_b = transposes(b)
-            regroup(a, pts_a)
-            regroup(b, pts_b)
-            quant(a)
-            quant(b)
-
         gate(0)
         gate(1)
-        up(0)
-        up(1)
+        up(0, None)
+        up(1, None)
+        regroup(0, transposes(0))
         for c in range(2, NCH):
             gate(c)
-            up(c)
-            if c % 2 == 0:
-                turn(c - 2, c - 1)
+            up(c, c - 2)
+            if c <= NCH - 2:
+                regroup(c - 1, transposes(c - 1))
 
         outs = {}
 
-        def stage2(m, gs):
+        def stage2(m, order):
             for n in range(2):
                 if (m, n) not in outs:
                     outs[(m, n)] = bank([P, 512], F32, "po")
-            for g in gs:
-                for n in range(2):
+            for g, n in order:
+                if True:
                     nc.tensor.matmul_mx(
                         out=outs[(m, n)][:],
                         lhsT=hq[g][:, m * P : (m + 1) * P].bitcast(FP8X4),
@@ -279,16 +277,21 @@ def tile_mlp_kernel(tc, x, gate_words, gate_scales, up_words, up_scales, down_wo
         def store(m):
             for n in range(2):
                 o = work.tile([P, 512], F32, name="o", tag="o", bufs=4)
-                if n == 0:
+                if n == m:
                     nc.vector.tensor_copy(out=o[:], in_=outs[(m, n)][:])
                 else:
                     nc.scalar.copy(out=o[:], in_=outs[(m, n)][:])
                 nc.sync.dma_start(out=out[m * P : (m + 1) * P, n * 512 : (n + 1) * 512], in_=o[:])
 
-        early = list(range(NCH // 2))
-        late = list(range(NCH // 2, NCH))
+        early = [(g, n) for g in range(NCH // 2) for n in range(2)]
+        late = [(g, n) for n in range(2) for g in range(NCH // 2, NCH)]
         stage2(0, early)
-        turn(NCH - 2, NCH - 1)
+        pts6 = transposes(NCH - 2)
+        pts7 = transposes(NCH - 1)
+        regroup(NCH - 2, pts6)
+        regroup(NCH - 1, pts7)
+        quant(NCH - 2)
+        quant(NCH - 1)
         stage2(1, early)
         stage2(0, late)
         store(0)

@@ -96,7 +96,7 @@ def tile_mlp_kernel(tc, x, gate_words, gate_scales, up_words, up_scales, down_wo
             )
 
         for m in range(MT):
-            nc.scalar.dma_start(out=x_sb[:, m, :], in_=x[m * P : (m + 1) * P, :])
+            nc.sync.dma_start(out=x_sb[:, m, :], in_=x[m * P : (m + 1) * P, :])
         nc.vector.memset(wz[:], 0.0)
         make_identity(nc, ident_f[:])
         nc.scalar.activation(out=warm_out[:], in_=wz[:, 0:1], func=SILU)

from contextlib import ExitStack

import concourse.mybir as mybir
from concourse.masks import make_identity

F32 = mybir.dt.float32
BF16 = mybir.dt.bfloat16
I32 = mybir.dt.int32
U32 = mybir.dt.uint32
U8 = mybir.dt.uint8
FP8X4 = mybir.dt.float8_e4m3fn_x4
FP4X4 = mybir.dt.float4_e2m1fn_x4
SILU = mybir.ActivationFunctionType.Silu
MULT = mybir.AluOpType.mult

P = 128
M, D, F = 256, 1024, 4096
MT = M // P
GD = D // 512
NCH = F // 512
FLOPS = 2 * M * D * F * 2 + 2 * M * F * D

DUMMIES_BEFORE = 5
DUMMIES_AFTER = 1


def tile_mlp_kernel(tc, x, gate_words, gate_scales, up_words, up_scales, down_words, down_scales, out):
    nc = tc.nc
    with ExitStack() as ctx:
        keep = ctx.enter_context(tc.tile_pool(name="keep", bufs=1))
        work = ctx.enter_context(tc.tile_pool(name="work", bufs=3))
        psum = ctx.enter_context(tc.psum_pool(name="psum", bufs=1))
        ctx.enter_context(tc.manual_schedule())

        taken = []

        def bank(shape, dtype, name):
            tag = "b%d" % (len(taken) % 8)
            taken.append(name)
            return psum.tile(shape, dtype, name=name, tag=tag)

        x_sb = keep.tile([P, MT, D], BF16, name="x_sb")
        ident_f = keep.tile([P, P], F32, name="ident_f")
        ident_b = keep.tile([P, P], BF16, name="ident_b")
        wz = keep.tile([P, 512], BF16, name="wz")
        warm_out = keep.tile([P, 1], F32, name="warm_out")
        xg = keep.tile([P, MT, GD, P * 4], BF16, name="xg", align_bytes=64)
        xq = keep.tile([P, MT, GD, P], U32, name="xq", align_bytes=64)
        xs = keep.tile([P, MT, GD, P], U8, name="xs", align_bytes=64)

        groups = [(0, 2), (2, 2), (4, 2), (6, 2)]
        planes = {}
        for i, (c0, n) in enumerate(groups):
            for w in range(2):
                planes[(i, w)] = keep.tile([P, GD, n * 512], U8, name="plane%d_%d" % (i, w), align_bytes=64)
        planes_d = []
        for i in range(2):
            planes_d.append(keep.tile([P, NCH // 2, D], U8, name="plane_d%d" % i, align_bytes=64))

        pieces = [(0, 1), (1, 1), (2, 1), (3, 1), (4, 1), (5, 1), (6, 2)]
        words = {}
        for j, (c0, n) in enumerate(pieces):
            for w in range(2):
                words[(j, w)] = keep.tile([P, GD, n * 1024], U8, name="words%d_%d" % (j, w), align_bytes=64)
        words_d = []
        for gg in range(NCH // 2):
            words_d.append(keep.tile([P, 2, 2 * D], U8, name="words_d%d" % gg, align_bytes=64))

        hq = []
        hs = []
        for c in range(NCH):
            hq.append(keep.tile([P, M], U32, name="hq%d" % c, align_bytes=64))
            hs.append(keep.tile([P, M], U8, name="hs%d" % c, align_bytes=64))

        def zero(plane):
            nc.vector.memset(plane[:].rearrange("p a b -> p (a b)").bitcast(I32), 0)

        w_dram = [gate_words.bitcast(I32), up_words.bitcast(I32)]
        s_dram = [gate_scales.bitcast(I32), up_scales.bitcast(I32)]

        def load_scales(i, w):
            c0, n = groups[i]
            pl = planes[(i, w)][:].bitcast(I32)
            a, b = c0 * 128, (c0 + n) * 128
            for r in range(4):
                nc.sync.dma_start(
                    out=pl[r:P:32, :, :],
                    in_=s_dram[w][:, r:16:4, a:b].rearrange("g q n -> q g n"),
                )

        def load_words(j, w):
            c0, n = pieces[j]
            nc.sync.dma_start(
                out=words[(j, w)][:].bitcast(I32),
                in_=w_dram[w][:, :, c0 * 256 : (c0 + n) * 256].rearrange("g p b -> p g b"),
            )

        for m in range(MT):
            nc.sync.dma_start(out=x_sb[:, m, :], in_=x[m * P : (m + 1) * P, :])
        nc.vector.memset(wz[:], 0.0)
        make_identity(nc, ident_f[:])
        nc.scalar.activation(out=warm_out[:], in_=wz[:, 0:1], func=SILU)

        pdum = bank([P, 512], F32, "pdum")

        def dummies(n):
            for i in range(n):
                nc.tensor.matmul(out=pdum[:], lhsT=wz[:, 0:P], rhs=wz[:], start=True, stop=True)

        dummies(DUMMIES_BEFORE)

        zero(planes[(0, 0)])
        zero(planes[(0, 1)])
        nc.vector.tensor_copy(out=ident_b[:], in_=ident_f[:])
        zero(planes[(1, 0)])
        zero(planes[(1, 1)])

        load_scales(0, 0)
        for g in range(GD):
            nc.sync.dma_start(out=words[(0, 0)][:, g, :].bitcast(I32), in_=w_dram[0][g, :, 0:256])
        load_words(1, 0)
        load_scales(0, 1)
        load_words(0, 1)
        load_words(1, 1)
        for w in range(2):
            load_scales(1, w)
            load_words(2, w)
        for w in range(2):
            load_words(3, w)

        for m in range(MT):
            xw = x_sb[:, m, :].bitcast(F32)
            for g in range(GD):
                xt = bank([P, 2, P], F32, "xt")
                for u in range(2):
                    nc.tensor.transpose(xt[:, u, :], xw[:, 256 * g + u : 256 * (g + 1) : 2], ident_f[:])
                dst = xg[:, m, g, :].bitcast(F32).rearrange("p (w u) -> p w u", u=2)
                src = xt[:].rearrange("p u w -> p w u")
                if g == 0:
                    nc.vector.tensor_copy(out=dst, in_=src)
                else:
                    nc.scalar.copy(out=dst, in_=src)
            for g in range(GD):
                nc.vector.quantize_mx(
                    out=xq[:, m, g, :].bitcast(FP8X4),
                    scales=xs[:, m, g, :],
                    in_=xg[:, m, g, :],
                )
        dummies(DUMMIES_AFTER)

        for i in (2, 3):
            for w in range(2):
                zero(planes[(i, w)])
        for i in range(2):
            zero(planes_d[i])
        for w in range(2):
            load_scales(2, w)
            load_words(4, w)
        for w in range(2):
            load_words(5, w)
        for w in range(2):
            load_scales(3, w)
            load_words(6, w)
        sd = down_scales.bitcast(I32)
        wd = down_words.bitcast(I32)
        for i in range(2):
            pd = planes_d[i][:].bitcast(I32)
            for r in range(4):
                nc.sync.dma_start(
                    out=pd[r:P:32, :, :],
                    in_=sd[4 * i : 4 * i + 4, r:16:4, :].rearrange("g q n -> q g n"),
                )
            for gg in (2 * i, 2 * i + 1):
                nc.sync.dma_start(
                    out=words_d[gg][:].bitcast(I32),
                    in_=wd[2 * gg : 2 * gg + 2, :, :].rearrange("g p b -> p g b"),
                )

        def find(table, c):
            for i, (c0, n) in enumerate(table):
                if c0 <= c < c0 + n:
                    return i, c - c0
            raise ValueError("no entry")

        h_tiles = {}
        grp_tiles = {}
        sil_tiles = {}

        def passes(c, w):
            i, ci = find(groups, c)
            j, cj = find(pieces, c)
            accs = []
            for m in range(MT):
                acc = bank([P, 512], F32, "acc")
                for g in range(GD):
                    nc.tensor.matmul_mx(
                        out=acc[:],
                        lhsT=xq[:, m, g, :].bitcast(FP8X4),
                        lhsT_scale=xs[:, m, g, :],
                        rhs=words[(j, w)][:, g, cj * 1024 : (cj + 1) * 1024].bitcast(FP4X4),
                        rhs_scale=planes[(i, w)][:, g, ci * 512 : (ci + 1) * 512],
                        start=(g == 0),
                        stop=(g == GD - 1),
                    )
                accs.append(acc)
            return accs

        def quant(c):
            nc.vector.quantize_mx(
                out=hq[c][:].bitcast(FP8X4),
                scales=hs[c][:],
                in_=grp_tiles[c][:].rearrange("p m w t -> p (m w t)"),
            )

        def gate(c):
            pg = passes(c, 0)
            for m in range(MT):
                s = work.tile([P, 4, P], F32, name="sil", tag="sil", bufs=4)
                nc.scalar.activation(out=s[:], in_=pg[m][:].rearrange("p (q t) -> p t q", t=4), func=SILU)
                sil_tiles[(c, m)] = s

        def up(c, quant_c):
            pu = passes(c, 1)
            for m in range(MT):
                h = work.tile([P, 4, P], BF16, name="h", tag="h", bufs=8)
                nc.vector.tensor_tensor(
                    out=h[:], in0=pu[m][:].rearrange("p (q t) -> p t q", t=4), in1=sil_tiles[(c, m)][:], op=MULT
                )
                h_tiles[(c, m)] = h
                if m == 0 and quant_c is not None:
                    quant(quant_c)

        def transposes(c):
            pts = []
            for m in range(MT):
                pt = bank([P, 4, P], BF16, "pt")
                for t in range(4):
                    nc.tensor.transpose(pt[:, t, :], h_tiles[(c, m)][:, t, :], ident_b[:])
                pts.append(pt)
            return pts

        def regroup(c, pts):
            grp = work.tile([P, MT, P, 4], BF16, name="grp", tag="grp", bufs=3, align_bytes=64)
            grp_tiles[c] = grp
            nc.scalar.copy(out=grp[:, 0, :, :], in_=pts[0][:].rearrange("p t w -> p w t"))
            nc.vector.tensor_copy(out=grp[:, 1, :, :], in_=pts[1][:].rearrange("p t w -> p w t"))

        gate(0)
        gate(1)
        up(0, None)
        up(1, None)
        regroup(0, transposes(0))
        for c in range(2, NCH):
            gate(c)
            up(c, c - 2)
            if c <= NCH - 2:
                regroup(c - 1, transposes(c - 1))

        outs = {}

        def stage2(m, order):
            for n in range(2):
                if (m, n) not in outs:
                    outs[(m, n)] = bank([P, 512], F32, "po")
            for g, n in order:
                if True:
                    nc.tensor.matmul_mx(
                        out=outs[(m, n)][:],
                        lhsT=hq[g][:, m * P : (m + 1) * P].bitcast(FP8X4),
                        lhsT_scale=hs[g][:, m * P : (m + 1) * P],
                        rhs=words_d[g // 2][:, g % 2, n * 1024 : (n + 1) * 1024].bitcast(FP4X4),
                        rhs_scale=planes_d[g // 4][:, g % 4, n * 512 : (n + 1) * 512],
                        start=(g == 0),
                        stop=(g == NCH - 1),
                    )

        def store(m):
            for n in range(2):
                o = work.tile([P, 512], F32, name="o", tag="o", bufs=4)
                if n == m:
                    nc.vector.tensor_copy(out=o[:], in_=outs[(m, n)][:])
                else:
                    nc.scalar.copy(out=o[:], in_=outs[(m, n)][:])
                nc.sync.dma_start(out=out[m * P : (m + 1) * P, n * 512 : (n + 1) * 512], in_=o[:])

        early = [(g, n) for g in range(NCH // 2) for n in range(2)]
        late = [(g, n) for n in range(2) for g in range(NCH // 2, NCH)]
        stage2(0, early)
        pts6 = transposes(NCH - 2)
        pts7 = transposes(NCH - 1)
        regroup(NCH - 2, pts6)
        regroup(NCH - 1, pts7)
        quant(NCH - 2)
        quant(NCH - 1)
        stage2(1, early)
        stage2(0, late)
        store(0)
        stage2(1, late)
        store(1)
